import numpy as np
import ml_dtypes

BF16 = ml_dtypes.bfloat16


def bf(x):
    return np.asarray(x, np.float32).astype(BF16)


def f32(x):
    return np.asarray(x, np.float32)


def f64(x):
    return np.asarray(x).astype(np.float64)


def striped(idx):
    return np.tile(idx.reshape(-1, 16).T, (8, 1))


C, S, D, K, N = 256, 2048, 512, 16, 8192


def setup_inputs():
    idx = np.concatenate([np.random.permutation(S) for _ in range(N // S)])
    return {"x": f32(np.random.standard_normal((C, S))), "w": f32(np.random.standard_normal((1, N)) * np.sqrt(2.0 / K)), "b": f32(0.1 * np.random.standard_normal((1, D))), "offs": striped(idx)}


def reference(x, w, b, offs):
    idx = offs[:16].T.reshape(-1)
    prod = f64(x)[:, idx] * f64(w)
    return np.maximum(prod.reshape(C, D, K).sum(axis=2) + f64(b), 0.0)

@@ -1,0 +1,58 @@
+import concourse.mybir as mybir
+
+F32 = mybir.dt.float32
+U16 = mybir.dt.uint16
+
+P = 128
+SAMPLES, IN_NODES = 256, 2048
+OUT_NODES, FAN_IN = 512, 16
+LIST = OUT_NODES * FAN_IN
+PIECE = 2048
+PIECE_NODES = PIECE // FAN_IN
+
+
+def tile_lcn_kernel(tc, x, w, b, offs, out):
+    nc = tc.nc
+    with (
+        tc.tile_pool(name="held", bufs=1) as held,
+        tc.tile_pool(name="work", bufs=2) as work,
+    ):
+        offsets = held.tile([P, LIST // 16], U16, name="offsets")
+        nc.sync.dma_start(offsets[:], offs)
+
+        tables = []
+        for block in range(SAMPLES // P):
+            table = held.tile([P, IN_NODES], F32, name=f"table{block}")
+            nc.sync.dma_start(table[:], x[block * P : (block + 1) * P, :])
+            tables.append(table)
+
+        weights = held.tile([P, LIST], F32, name="weights")
+        for piece in range(LIST // PIECE):
+            entries = slice(piece * PIECE, (piece + 1) * PIECE)
+            nc.scalar.dma_start(weights[:, entries], w[0, entries].partition_broadcast(P))
+        bias = held.tile([P, OUT_NODES], F32, name="bias")
+        nc.scalar.dma_start(bias[:], b[0, :].partition_broadcast(P))
+
+        for block in range(SAMPLES // P):
+            sums = work.tile([P, OUT_NODES], F32, name="sums")
+            for piece in range(LIST // PIECE):
+                entries = slice(piece * PIECE, (piece + 1) * PIECE)
+                nodes = slice(piece * PIECE_NODES, (piece + 1) * PIECE_NODES)
+                product = work.tile([P, PIECE], F32, name="product")
+                nc.vector.tensor_tensor(
+                    product[:],
+                    tables[block][:].indirect(offsets[:, piece * (PIECE // 16) : (piece + 1) * (PIECE // 16)]),
+                    weights[:, entries],
+                    mybir.AluOpType.mult,
+                )
+                nc.vector.tensor_reduce(
+                    sums[:, nodes],
+                    product[:].rearrange("p (d k) -> p d k", k=FAN_IN),
+                    axis=mybir.AxisListType.X,
+                    op=mybir.AluOpType.add,
+                )
+            biased = work.tile([P, OUT_NODES], F32, name="biased")
+            nc.vector.tensor_tensor(biased[:], sums[:], bias[:], mybir.AluOpType.add)
+            result = work.tile([P, OUT_NODES], F32, name="result")
+            nc.scalar.activation(result[:], biased[:], mybir.ActivationFunctionType.Relu)
+            nc.sync.dma_start(out[block * P : (block + 1) * P, :], result[:])

@@ -1,4 +1,5 @@
 import concourse.mybir as mybir
+from concourse.masks import make_identity
 
 F32 = mybir.dt.float32
 U16 = mybir.dt.uint16
@@ -10,12 +11,15 @@ LIST = OUT_NODES * FAN_IN
 PIECE = 2048
 PIECE_NODES = PIECE // FAN_IN
 
+FLOPS = 2 * SAMPLES * LIST
+
 
 def tile_lcn_kernel(tc, x, w, b, offs, out):
     nc = tc.nc
     with (
         tc.tile_pool(name="held", bufs=1) as held,
-        tc.tile_pool(name="work", bufs=2) as work,
+        tc.tile_pool(name="work", bufs=3) as work,
+        tc.psum_pool(name="psum", bufs=4) as psum,
     ):
         offsets = held.tile([P, LIST // 16], U16, name="offsets")
         nc.sync.dma_start(offsets[:], offs)
@@ -27,17 +31,21 @@ def tile_lcn_kernel(tc, x, w, b, offs, out):
             tables.append(table)
 
         weights = held.tile([P, LIST], F32, name="weights")
+        bias = held.tile([P, OUT_NODES], F32, name="bias")
         for piece in range(LIST // PIECE):
             entries = slice(piece * PIECE, (piece + 1) * PIECE)
             nc.scalar.dma_start(weights[:, entries], w[0, entries].partition_broadcast(P))
-        bias = held.tile([P, OUT_NODES], F32, name="bias")
-        nc.scalar.dma_start(bias[:], b[0, :].partition_broadcast(P))
+            if piece == 0:
+                nc.scalar.dma_start(bias[:], b[0, :].partition_broadcast(P))
+
+        identity = held.tile([P, P], F32, name="identity")
+        make_identity(nc, identity[:])
 
         for block in range(SAMPLES // P):
-            sums = work.tile([P, OUT_NODES], F32, name="sums")
             for piece in range(LIST // PIECE):
                 entries = slice(piece * PIECE, (piece + 1) * PIECE)
                 nodes = slice(piece * PIECE_NODES, (piece + 1) * PIECE_NODES)
+
                 product = work.tile([P, PIECE], F32, name="product")
                 nc.vector.tensor_tensor(
                     product[:],
@@ -45,14 +53,13 @@ def tile_lcn_kernel(tc, x, w, b, offs, out):
                     weights[:, entries],
                     mybir.AluOpType.mult,
                 )
-                nc.vector.tensor_reduce(
-                    sums[:, nodes],
-                    product[:].rearrange("p (d k) -> p d k", k=FAN_IN),
-                    axis=mybir.AxisListType.X,
-                    op=mybir.AluOpType.add,
-                )
-            biased = work.tile([P, OUT_NODES], F32, name="biased")
-            nc.vector.tensor_tensor(biased[:], sums[:], bias[:], mybir.AluOpType.add)
-            result = work.tile([P, OUT_NODES], F32, name="result")
-            nc.scalar.activation(result[:], biased[:], mybir.ActivationFunctionType.Relu)
-            nc.sync.dma_start(out[block * P : (block + 1) * P, :], result[:])
+
+                by_neighbour = product[:].rearrange("p (d k) -> p d k", k=FAN_IN)
+                total = psum.tile([P, PIECE_NODES], F32, name="total")
+                nc.tensor.matmul(total[:], identity[:], bias[:, nodes], start=True, stop=False)
+                for k in range(FAN_IN):
+                    nc.tensor.matmul(total[:], identity[:], by_neighbour[:, :, k], start=False, stop=(k == FAN_IN - 1))
+
+                result = work.tile([P, PIECE_NODES], F32, name="result")
+                nc.scalar.activation(result[:], total[:], mybir.ActivationFunctionType.Relu)
+                nc.sync.dma_start(out[block * P : (block + 1) * P, nodes], result[:])

@@ -10,6 +10,8 @@ OUT_NODES, FAN_IN = 512, 16
 LIST = OUT_NODES * FAN_IN
 PIECE = 2048
 PIECE_NODES = PIECE // FAN_IN
+RUN = 4
+LAG = 2
 
 FLOPS = 2 * SAMPLES * LIST
 
@@ -18,8 +20,8 @@ def tile_lcn_kernel(tc, x, w, b, offs, out):
     nc = tc.nc
     with (
         tc.tile_pool(name="held", bufs=1) as held,
-        tc.tile_pool(name="work", bufs=3) as work,
-        tc.psum_pool(name="psum", bufs=4) as psum,
+        tc.tile_pool(name="work", bufs=LAG + 1) as work,
+        tc.psum_pool(name="psum", bufs=LAG + 2) as psum,
     ):
         offsets = held.tile([P, LIST // 16], U16, name="offsets")
         nc.sync.dma_start(offsets[:], offs)
@@ -41,25 +43,38 @@ def tile_lcn_kernel(tc, x, w, b, offs, out):
         identity = held.tile([P, P], F32, name="identity")
         make_identity(nc, identity[:])
 
-        for block in range(SAMPLES // P):
-            for piece in range(LIST // PIECE):
-                entries = slice(piece * PIECE, (piece + 1) * PIECE)
-                nodes = slice(piece * PIECE_NODES, (piece + 1) * PIECE_NODES)
+        jobs = [(block, piece) for block in range(SAMPLES // P) for piece in range(LIST // PIECE)]
+        partials = {}
 
-                product = work.tile([P, PIECE], F32, name="product")
-                nc.vector.tensor_tensor(
-                    product[:],
-                    tables[block][:].indirect(offsets[:, piece * (PIECE // 16) : (piece + 1) * (PIECE // 16)]),
-                    weights[:, entries],
-                    mybir.AluOpType.mult,
-                )
+        def multiply_and_fold(block, piece):
+            entries = slice(piece * PIECE, (piece + 1) * PIECE)
+            nodes = slice(piece * PIECE_NODES, (piece + 1) * PIECE_NODES)
+            product = work.tile([P, PIECE], F32, name="product")
+            nc.vector.tensor_tensor(
+                product[:],
+                tables[block][:].indirect(offsets[:, piece * (PIECE // 16) : (piece + 1) * (PIECE // 16)]),
+                weights[:, entries],
+                mybir.AluOpType.mult,
+            )
+            runs = product[:].rearrange("p (d m j) -> p m d j", m=FAN_IN // RUN, j=RUN)
+            partial = psum.tile([P, PIECE_NODES, RUN], F32, name="partial")
+            for m in range(FAN_IN // RUN):
+                nc.tensor.matmul(partial[:], identity[:], runs[:, m], start=(m == 0), stop=False)
+            nc.tensor.matmul(partial[:, :, 0], identity[:], bias[:, nodes], start=False, stop=True)
+            partials[(block, piece)] = partial
 
-                by_neighbour = product[:].rearrange("p (d k) -> p d k", k=FAN_IN)
-                total = psum.tile([P, PIECE_NODES], F32, name="total")
-                nc.tensor.matmul(total[:], identity[:], bias[:, nodes], start=True, stop=False)
-                for k in range(FAN_IN):
-                    nc.tensor.matmul(total[:], identity[:], by_neighbour[:, :, k], start=False, stop=(k == FAN_IN - 1))
+        def finish(block, piece):
+            nodes = slice(piece * PIECE_NODES, (piece + 1) * PIECE_NODES)
+            total = work.tile([P, PIECE_NODES], F32, name="total")
+            nc.vector.tensor_reduce(
+                total[:], partials[(block, piece)][:], axis=mybir.AxisListType.X, op=mybir.AluOpType.add
+            )
+            result = work.tile([P, PIECE_NODES], F32, name="result")
+            nc.scalar.activation(result[:], total[:], mybir.ActivationFunctionType.Relu)
+            nc.sync.dma_start(out[block * P : (block + 1) * P, nodes], result[:])
 
-                result = work.tile([P, PIECE_NODES], F32, name="result")
-                nc.scalar.activation(result[:], total[:], mybir.ActivationFunctionType.Relu)
-                nc.sync.dma_start(out[block * P : (block + 1) * P, nodes], result[:])
+        for step in range(len(jobs) + LAG):
+            if step < len(jobs):
+                multiply_and_fold(*jobs[step])
+            if step >= LAG:
+                finish(*jobs[step - LAG])

@@ -8,7 +8,7 @@ P = 128
 SAMPLES, IN_NODES = 256, 2048
 OUT_NODES, FAN_IN = 512, 16
 LIST = OUT_NODES * FAN_IN
-PIECE = 2048
+PIECE = 1024
 PIECE_NODES = PIECE // FAN_IN
 RUN = 4
 LAG = 2
@@ -37,7 +37,7 @@ def tile_lcn_kernel(tc, x, w, b, offs, out):
         for piece in range(LIST // PIECE):
             entries = slice(piece * PIECE, (piece + 1) * PIECE)
             nc.scalar.dma_start(weights[:, entries], w[0, entries].partition_broadcast(P))
-            if piece == 0:
+            if piece == 1:
                 nc.scalar.dma_start(bias[:], b[0, :].partition_broadcast(P))
 
         identity = held.tile([P, P], F32, name="identity")

@@ -10,7 +10,7 @@ OUT_NODES, FAN_IN = 512, 16
 LIST = OUT_NODES * FAN_IN
 PIECE = 1024
 PIECE_NODES = PIECE // FAN_IN
-RUN = 4
+RUN = 2
 LAG = 2
 
 FLOPS = 2 * SAMPLES * LIST

@@ -10,8 +10,8 @@ OUT_NODES, FAN_IN = 512, 16
 LIST = OUT_NODES * FAN_IN
 PIECE = 1024
 PIECE_NODES = PIECE // FAN_IN
-RUN = 2
-LAG = 2
+RUN = 4
+LAG = 6
 
 FLOPS = 2 * SAMPLES * LIST
 
@@ -20,7 +20,7 @@ def tile_lcn_kernel(tc, x, w, b, offs, out):
     nc = tc.nc
     with (
         tc.tile_pool(name="held", bufs=1) as held,
-        tc.tile_pool(name="work", bufs=LAG + 1) as work,
+        tc.tile_pool(name="work", bufs=LAG + 2) as work,
         tc.psum_pool(name="psum", bufs=LAG + 2) as psum,
     ):
         offsets = held.tile([P, LIST // 16], U16, name="offsets")
@@ -56,11 +56,12 @@ def tile_lcn_kernel(tc, x, w, b, offs, out):
                 weights[:, entries],
                 mybir.AluOpType.mult,
             )
+            firsts = product[:].rearrange("p (d k) -> p d k", k=FAN_IN)[:, :, 0]
+            nc.gpsimd.tensor_tensor(firsts, firsts, bias[:, nodes], mybir.AluOpType.add)
             runs = product[:].rearrange("p (d m j) -> p m d j", m=FAN_IN // RUN, j=RUN)
             partial = psum.tile([P, PIECE_NODES, RUN], F32, name="partial")
-            for m in range(FAN_IN // RUN):
-                nc.tensor.matmul(partial[:], identity[:], runs[:, m], start=(m == 0), stop=False)
-            nc.tensor.matmul(partial[:, :, 0], identity[:], bias[:, nodes], start=False, stop=True)
+            for m in range(FAN_IN // RUN - 1, -1, -1):
+                nc.tensor.matmul(partial[:], identity[:], runs[:, m], start=(m == FAN_IN // RUN - 1), stop=(m == 0))
             partials[(block, piece)] = partial
 
         def finish(block, piece):

@@ -7,11 +7,12 @@ U16 = mybir.dt.uint16
 P = 128
 SAMPLES, IN_NODES = 256, 2048
 OUT_NODES, FAN_IN = 512, 16
+BLOCKS = SAMPLES // P
 LIST = OUT_NODES * FAN_IN
 PIECE = 1024
 PIECE_NODES = PIECE // FAN_IN
 RUN = 4
-LAG = 6
+RUNS = FAN_IN // RUN
 
 FLOPS = 2 * SAMPLES * LIST
 
@@ -20,62 +21,48 @@ def tile_lcn_kernel(tc, x, w, b, offs, out):
     nc = tc.nc
     with (
         tc.tile_pool(name="held", bufs=1) as held,
-        tc.tile_pool(name="work", bufs=LAG + 2) as work,
-        tc.psum_pool(name="psum", bufs=LAG + 2) as psum,
+        tc.tile_pool(name="work", bufs=3) as work,
+        tc.psum_pool(name="psum", bufs=4) as psum,
     ):
         offsets = held.tile([P, LIST // 16], U16, name="offsets")
         nc.sync.dma_start(offsets[:], offs)
 
-        tables = []
-        for block in range(SAMPLES // P):
-            table = held.tile([P, IN_NODES], F32, name=f"table{block}")
-            nc.sync.dma_start(table[:], x[block * P : (block + 1) * P, :])
-            tables.append(table)
+        tables = [held.tile([P, IN_NODES], F32, name=f"table{block}") for block in range(BLOCKS)]
+        bias = held.tile([P, OUT_NODES], F32, name="bias")
+        nc.sync.dma_start(tables[0][:], x[0:P, :])
+        nc.sync.dma_start(bias[:], b[0, :].partition_broadcast(P))
+        for block in range(1, BLOCKS):
+            nc.sync.dma_start(tables[block][:], x[block * P : (block + 1) * P, :])
 
         weights = held.tile([P, LIST], F32, name="weights")
-        bias = held.tile([P, OUT_NODES], F32, name="bias")
         for piece in range(LIST // PIECE):
             entries = slice(piece * PIECE, (piece + 1) * PIECE)
             nc.scalar.dma_start(weights[:, entries], w[0, entries].partition_broadcast(P))
-            if piece == 1:
-                nc.scalar.dma_start(bias[:], b[0, :].partition_broadcast(P))
 
         identity = held.tile([P, P], F32, name="identity")
         make_identity(nc, identity[:])
 
-        jobs = [(block, piece) for block in range(SAMPLES // P) for piece in range(LIST // PIECE)]
-        partials = {}
+        for block in range(BLOCKS):
+            for piece in range(LIST // PIECE):
+                entries = slice(piece * PIECE, (piece + 1) * PIECE)
+                nodes = slice(piece * PIECE_NODES, (piece + 1) * PIECE_NODES)
 
-        def multiply_and_fold(block, piece):
-            entries = slice(piece * PIECE, (piece + 1) * PIECE)
-            nodes = slice(piece * PIECE_NODES, (piece + 1) * PIECE_NODES)
-            product = work.tile([P, PIECE], F32, name="product")
-            nc.vector.tensor_tensor(
-                product[:],
-                tables[block][:].indirect(offsets[:, piece * (PIECE // 16) : (piece + 1) * (PIECE // 16)]),
-                weights[:, entries],
-                mybir.AluOpType.mult,
-            )
-            firsts = product[:].rearrange("p (d k) -> p d k", k=FAN_IN)[:, :, 0]
-            nc.gpsimd.tensor_tensor(firsts, firsts, bias[:, nodes], mybir.AluOpType.add)
-            runs = product[:].rearrange("p (d m j) -> p m d j", m=FAN_IN // RUN, j=RUN)
-            partial = psum.tile([P, PIECE_NODES, RUN], F32, name="partial")
-            for m in range(FAN_IN // RUN - 1, -1, -1):
-                nc.tensor.matmul(partial[:], identity[:], runs[:, m], start=(m == FAN_IN // RUN - 1), stop=(m == 0))
-            partials[(block, piece)] = partial
+                product = work.tile([P, PIECE], F32, name="product")
+                nc.vector.tensor_tensor(
+                    product[:],
+                    tables[block][:].indirect(offsets[:, piece * (PIECE // 16) : (piece + 1) * (PIECE // 16)]),
+                    weights[:, entries],
+                    mybir.AluOpType.mult,
+                )
 
-        def finish(block, piece):
-            nodes = slice(piece * PIECE_NODES, (piece + 1) * PIECE_NODES)
-            total = work.tile([P, PIECE_NODES], F32, name="total")
-            nc.vector.tensor_reduce(
-                total[:], partials[(block, piece)][:], axis=mybir.AxisListType.X, op=mybir.AluOpType.add
-            )
-            result = work.tile([P, PIECE_NODES], F32, name="result")
-            nc.scalar.activation(result[:], total[:], mybir.ActivationFunctionType.Relu)
-            nc.sync.dma_start(out[block * P : (block + 1) * P, nodes], result[:])
+                runs = product[:].rearrange("p (d m j) -> p m d j", m=RUNS, j=RUN)
+                partial = psum.tile([P, PIECE_NODES, RUN], F32, name="partial")
+                for m in range(RUNS):
+                    nc.tensor.matmul(partial[:], identity[:], runs[:, m], start=(m == 0), stop=False)
+                nc.tensor.matmul(partial[:, :, 0], identity[:], bias[:, nodes], start=False, stop=True)
 
-        for step in range(len(jobs) + LAG):
-            if step < len(jobs):
-                multiply_and_fold(*jobs[step])
-            if step >= LAG:
-                finish(*jobs[step - LAG])
+                total = work.tile([P, PIECE_NODES], F32, name="total")
+                nc.vector.tensor_reduce(total[:], partial[:], axis=mybir.AxisListType.X, op=mybir.AluOpType.add)
+                result = work.tile([P, PIECE_NODES], F32, name="result")
+                nc.scalar.activation(result[:], total[:], mybir.ActivationFunctionType.Relu)
+                nc.sync.dma_start(out[block * P : (block + 1) * P, nodes], result[:])

@@ -1,5 +1,5 @@
 import concourse.mybir as mybir
-from concourse.masks import make_identity
+from concourse.masks import make_block_diagonal, make_identity
 
 F32 = mybir.dt.float32
 U16 = mybir.dt.uint16
@@ -9,10 +9,10 @@ SAMPLES, IN_NODES = 256, 2048
 OUT_NODES, FAN_IN = 512, 16
 BLOCKS = SAMPLES // P
 LIST = OUT_NODES * FAN_IN
-PIECE = 1024
-PIECE_NODES = PIECE // FAN_IN
-RUN = 4
-RUNS = FAN_IN // RUN
+HALVES = 2
+PIECE_NODES = P // HALVES
+PIECE = PIECE_NODES * FAN_IN
+STEP = FAN_IN // HALVES
 
 FLOPS = 2 * SAMPLES * LIST
 
@@ -22,7 +22,7 @@ def tile_lcn_kernel(tc, x, w, b, offs, out):
     with (
         tc.tile_pool(name="held", bufs=1) as held,
         tc.tile_pool(name="work", bufs=3) as work,
-        tc.psum_pool(name="psum", bufs=4) as psum,
+        tc.psum_pool(name="psum", bufs=2) as psum,
     ):
         offsets = held.tile([P, LIST // 16], U16, name="offsets")
         nc.sync.dma_start(offsets[:], offs)
@@ -41,6 +41,9 @@ def tile_lcn_kernel(tc, x, w, b, offs, out):
 
         identity = held.tile([P, P], F32, name="identity")
         make_identity(nc, identity[:])
+        blocks_of_ones = held.tile([P, P], F32, name="blocks_of_ones")
+        make_block_diagonal(nc, blocks_of_ones[:], HALVES)
+        pair_of = blocks_of_ones[:].rearrange("q (d h) -> q d h", h=HALVES)[:, :, 0]
 
         for block in range(BLOCKS):
             for piece in range(LIST // PIECE):
@@ -55,14 +58,18 @@ def tile_lcn_kernel(tc, x, w, b, offs, out):
                     mybir.AluOpType.mult,
                 )
 
-                runs = product[:].rearrange("p (d m j) -> p m d j", m=RUNS, j=RUN)
-                partial = psum.tile([P, PIECE_NODES, RUN], F32, name="partial")
-                for m in range(RUNS):
-                    nc.tensor.matmul(partial[:], identity[:], runs[:, m], start=(m == 0), stop=False)
-                nc.tensor.matmul(partial[:, :, 0], identity[:], bias[:, nodes], start=False, stop=True)
+                every_step = product[:].rearrange("p (q k) -> p q k", k=STEP)
+                halves = psum.tile([P, P], F32, name="halves")
+                for k in range(STEP):
+                    nc.tensor.matmul(
+                        halves[:], every_step[:, :, k], identity[:], start=(k == 0), stop=(k == STEP - 1), is_transpose=True
+                    )
+                halves_sbuf = work.tile([P, P], F32, name="halves_sbuf")
+                nc.scalar.copy(halves_sbuf[:], halves[:])
 
-                total = work.tile([P, PIECE_NODES], F32, name="total")
-                nc.vector.tensor_reduce(total[:], partial[:], axis=mybir.AxisListType.X, op=mybir.AluOpType.add)
+                total = psum.tile([P, PIECE_NODES], F32, name="total")
+                nc.tensor.matmul(total[:], identity[:], bias[:, nodes], start=True, stop=False)
+                nc.tensor.matmul(total[:], halves_sbuf[:], pair_of, start=False, stop=True)
                 result = work.tile([P, PIECE_NODES], F32, name="result")
                 nc.scalar.activation(result[:], total[:], mybir.ActivationFunctionType.Relu)
                 nc.sync.dma_start(out[block * P : (block + 1) * P, nodes], result[:])

@@ -28,16 +28,17 @@ def tile_lcn_kernel(tc, x, w, b, offs, out):
         nc.sync.dma_start(offsets[:], offs)
 
         tables = [held.tile([P, IN_NODES], F32, name=f"table{block}") for block in range(BLOCKS)]
-        bias = held.tile([P, OUT_NODES], F32, name="bias")
-        nc.sync.dma_start(tables[0][:], x[0:P, :])
-        nc.sync.dma_start(bias[:], b[0, :].partition_broadcast(P))
-        for block in range(1, BLOCKS):
-            nc.sync.dma_start(tables[block][:], x[block * P : (block + 1) * P, :])
-
         weights = held.tile([P, LIST], F32, name="weights")
+        bias = held.tile([P, OUT_NODES], F32, name="bias")
         for piece in range(LIST // PIECE):
             entries = slice(piece * PIECE, (piece + 1) * PIECE)
-            nc.scalar.dma_start(weights[:, entries], w[0, entries].partition_broadcast(P))
+            if piece == 0:
+                nc.sync.dma_start(tables[0][:], x[0:P, :])
+            nc.sync.dma_start(weights[:, entries], w[0, entries].partition_broadcast(P))
+            if piece == 0:
+                for block in range(1, BLOCKS):
+                    nc.sync.dma_start(tables[block][:], x[block * P : (block + 1) * P, :])
+                nc.sync.dma_start(bias[:], b[0, :].partition_broadcast(P))
 
         identity = held.tile([P, P], F32, name="identity")
         make_identity(nc, identity[:])
@@ -45,8 +46,8 @@ def tile_lcn_kernel(tc, x, w, b, offs, out):
         make_block_diagonal(nc, blocks_of_ones[:], HALVES)
         pair_of = blocks_of_ones[:].rearrange("q (d h) -> q d h", h=HALVES)[:, :, 0]
 
-        for block in range(BLOCKS):
-            for piece in range(LIST // PIECE):
+        for piece in range(LIST // PIECE):
+            for block in range(BLOCKS):
                 entries = slice(piece * PIECE, (piece + 1) * PIECE)
                 nodes = slice(piece * PIECE_NODES, (piece + 1) * PIECE_NODES)
 

@@ -1,5 +1,5 @@
 import concourse.mybir as mybir
-from concourse.masks import make_block_diagonal, make_identity
+from concourse.masks import make_identity
 
 F32 = mybir.dt.float32
 U16 = mybir.dt.uint16
@@ -9,10 +9,9 @@ SAMPLES, IN_NODES = 256, 2048
 OUT_NODES, FAN_IN = 512, 16
 BLOCKS = SAMPLES // P
 LIST = OUT_NODES * FAN_IN
-HALVES = 2
-PIECE_NODES = P // HALVES
+PIECE_NODES = P
 PIECE = PIECE_NODES * FAN_IN
-STEP = FAN_IN // HALVES
+PIECES = LIST // PIECE
 
 FLOPS = 2 * SAMPLES * LIST
 
@@ -29,24 +28,21 @@ def tile_lcn_kernel(tc, x, w, b, offs, out):
 
         tables = [held.tile([P, IN_NODES], F32, name=f"table{block}") for block in range(BLOCKS)]
         weights = held.tile([P, LIST], F32, name="weights")
-        bias = held.tile([P, OUT_NODES], F32, name="bias")
-        for piece in range(LIST // PIECE):
+        nc.sync.dma_start(tables[0][:], x[0:P, :])
+        nc.sync.dma_start(weights[:, 0:PIECE], w[0, 0:PIECE].partition_broadcast(P))
+        for block in range(1, BLOCKS):
+            nc.sync.dma_start(tables[block][:], x[block * P : (block + 1) * P, :])
+        for piece in range(1, PIECES):
             entries = slice(piece * PIECE, (piece + 1) * PIECE)
-            if piece == 0:
-                nc.sync.dma_start(tables[0][:], x[0:P, :])
             nc.sync.dma_start(weights[:, entries], w[0, entries].partition_broadcast(P))
-            if piece == 0:
-                for block in range(1, BLOCKS):
-                    nc.sync.dma_start(tables[block][:], x[block * P : (block + 1) * P, :])
-                nc.sync.dma_start(bias[:], b[0, :].partition_broadcast(P))
+
+        bias = held.tile([P, PIECES], F32, name="bias")
+        nc.scalar.dma_start(bias[:], b.rearrange("o (a p) -> p (a o)", p=P))
 
         identity = held.tile([P, P], F32, name="identity")
         make_identity(nc, identity[:])
-        blocks_of_ones = held.tile([P, P], F32, name="blocks_of_ones")
-        make_block_diagonal(nc, blocks_of_ones[:], HALVES)
-        pair_of = blocks_of_ones[:].rearrange("q (d h) -> q d h", h=HALVES)[:, :, 0]
 
-        for piece in range(LIST // PIECE):
+        for piece in range(PIECES):
             for block in range(BLOCKS):
                 entries = slice(piece * PIECE, (piece + 1) * PIECE)
                 nodes = slice(piece * PIECE_NODES, (piece + 1) * PIECE_NODES)
@@ -59,18 +55,20 @@ def tile_lcn_kernel(tc, x, w, b, offs, out):
                     mybir.AluOpType.mult,
                 )
 
-                every_step = product[:].rearrange("p (q k) -> p q k", k=STEP)
-                halves = psum.tile([P, P], F32, name="halves")
-                for k in range(STEP):
+                by_neighbour = product[:].rearrange("p (q k) -> p q k", k=FAN_IN)
+                sums = psum.tile([P, P], F32, name="sums")
+                for k in range(FAN_IN):
                     nc.tensor.matmul(
-                        halves[:], every_step[:, :, k], identity[:], start=(k == 0), stop=(k == STEP - 1), is_transpose=True
+                        sums[:], by_neighbour[:, :, k], identity[:], start=(k == 0), stop=(k == FAN_IN - 1), is_transpose=True
                     )
-                halves_sbuf = work.tile([P, P], F32, name="halves_sbuf")
-                nc.scalar.copy(halves_sbuf[:], halves[:])
 
-                total = psum.tile([P, PIECE_NODES], F32, name="total")
-                nc.tensor.matmul(total[:], identity[:], bias[:, nodes], start=True, stop=False)
-                nc.tensor.matmul(total[:], halves_sbuf[:], pair_of, start=False, stop=True)
-                result = work.tile([P, PIECE_NODES], F32, name="result")
-                nc.scalar.activation(result[:], total[:], mybir.ActivationFunctionType.Relu)
+                active = work.tile([P, P], F32, name="active")
+                nc.scalar.activation(
+                    active[:], sums[:], mybir.ActivationFunctionType.Relu, bias=bias[:, piece : piece + 1]
+                )
+
+                turned = psum.tile([P, P], F32, name="turned")
+                nc.tensor.transpose(turned[:], active[:], identity[:])
+                result = work.tile([P, P], F32, name="result")
+                nc.scalar.copy(result[:], turned[:])
                 nc.sync.dma_start(out[block * P : (block + 1) * P, nodes], result[:])

@@ -12,6 +12,8 @@ LIST = OUT_NODES * FAN_IN
 PIECE_NODES = P
 PIECE = PIECE_NODES * FAN_IN
 PIECES = LIST // PIECE
+FIRST_CUT = ((0, PIECE_NODES // 4), (PIECE_NODES // 4, PIECE_NODES // 4), (PIECE_NODES // 2, PIECE_NODES // 2))
+WHOLE = ((0, PIECE_NODES),)
 
 FLOPS = 2 * SAMPLES * LIST
 
@@ -29,7 +31,9 @@ def tile_lcn_kernel(tc, x, w, b, offs, out):
         tables = [held.tile([P, IN_NODES], F32, name=f"table{block}") for block in range(BLOCKS)]
         weights = held.tile([P, LIST], F32, name="weights")
         nc.sync.dma_start(tables[0][:], x[0:P, :])
-        nc.sync.dma_start(weights[:, 0:PIECE], w[0, 0:PIECE].partition_broadcast(P))
+        for first_node, nodes in FIRST_CUT:
+            entries = slice(first_node * FAN_IN, (first_node + nodes) * FAN_IN)
+            nc.sync.dma_start(weights[:, entries], w[0, entries].partition_broadcast(P))
         for block in range(1, BLOCKS):
             nc.sync.dma_start(tables[block][:], x[block * P : (block + 1) * P, :])
         for piece in range(1, PIECES):
@@ -44,16 +48,15 @@ def tile_lcn_kernel(tc, x, w, b, offs, out):
 
         for piece in range(PIECES):
             for block in range(BLOCKS):
-                entries = slice(piece * PIECE, (piece + 1) * PIECE)
-                nodes = slice(piece * PIECE_NODES, (piece + 1) * PIECE_NODES)
-
                 product = work.tile([P, PIECE], F32, name="product")
-                nc.vector.tensor_tensor(
-                    product[:],
-                    tables[block][:].indirect(offsets[:, piece * (PIECE // 16) : (piece + 1) * (PIECE // 16)]),
-                    weights[:, entries],
-                    mybir.AluOpType.mult,
-                )
+                for first_node, nodes in FIRST_CUT if (piece, block) == (0, 0) else WHOLE:
+                    node = piece * PIECE_NODES + first_node
+                    nc.vector.tensor_tensor(
+                        product[:, first_node * FAN_IN : (first_node + nodes) * FAN_IN],
+                        tables[block][:].indirect(offsets[:, node : node + nodes]),
+                        weights[:, node * FAN_IN : (node + nodes) * FAN_IN],
+                        mybir.AluOpType.mult,
+                    )
 
                 by_neighbour = product[:].rearrange("p (q k) -> p q k", k=FAN_IN)
                 sums = psum.tile([P, P], F32, name="sums")
@@ -71,4 +74,4 @@ def tile_lcn_kernel(tc, x, w, b, offs, out):
                 nc.tensor.transpose(turned[:], active[:], identity[:])
                 result = work.tile([P, P], F32, name="result")
                 nc.scalar.copy(result[:], turned[:])
-                nc.sync.dma_start(out[block * P : (block + 1) * P, nodes], result[:])
+                nc.sync.dma_start(out[block * P : (block + 1) * P, piece * PIECE_NODES : (piece + 1) * PIECE_NODES], result[:])

@@ -12,6 +12,8 @@ LIST = OUT_NODES * FAN_IN
 PIECE_NODES = P
 PIECE = PIECE_NODES * FAN_IN
 PIECES = LIST // PIECE
+W_ROWS = LIST // P
+BANK = 512
 FIRST_CUT = ((0, PIECE_NODES // 4), (PIECE_NODES // 4, PIECE_NODES // 4), (PIECE_NODES // 2, PIECE_NODES // 2))
 WHOLE = ((0, PIECE_NODES),)
 
@@ -23,29 +25,40 @@ def tile_lcn_kernel(tc, x, w, b, offs, out):
     with (
         tc.tile_pool(name="held", bufs=1) as held,
         tc.tile_pool(name="work", bufs=3) as work,
+        tc.psum_pool(name="once", bufs=1) as once,
         tc.psum_pool(name="psum", bufs=2) as psum,
     ):
-        offsets = held.tile([P, LIST // 16], U16, name="offsets")
-        nc.sync.dma_start(offsets[:], offs)
-
-        tables = [held.tile([P, IN_NODES], F32, name=f"table{block}") for block in range(BLOCKS)]
-        weights = held.tile([P, LIST], F32, name="weights")
-        nc.sync.dma_start(tables[0][:], x[0:P, :])
-        for first_node, nodes in FIRST_CUT:
-            entries = slice(first_node * FAN_IN, (first_node + nodes) * FAN_IN)
-            nc.sync.dma_start(weights[:, entries], w[0, entries].partition_broadcast(P))
-        for block in range(1, BLOCKS):
-            nc.sync.dma_start(tables[block][:], x[block * P : (block + 1) * P, :])
-        for piece in range(1, PIECES):
-            entries = slice(piece * PIECE, (piece + 1) * PIECE)
-            nc.sync.dma_start(weights[:, entries], w[0, entries].partition_broadcast(P))
-
+        w_rows = held.tile([W_ROWS, P], F32, name="w_rows")
+        nc.scalar.dma_start(w_rows[:], w.rearrange("o (j p) -> (o j) p", p=P))
         bias = held.tile([P, PIECES], F32, name="bias")
         nc.scalar.dma_start(bias[:], b.rearrange("o (a p) -> p (a o)", p=P))
+
+        offsets = held.tile([P, LIST // 16], U16, name="offsets")
+        nc.sync.dma_start(offsets[:], offs)
+        tables = [held.tile([P, IN_NODES], F32, name=f"table{block}") for block in range(BLOCKS)]
+        for block in range(BLOCKS):
+            nc.sync.dma_start(tables[block][:], x[block * P : (block + 1) * P, :])
 
         identity = held.tile([P, P], F32, name="identity")
         make_identity(nc, identity[:])
 
+        w_flipped = once.tile([P, W_ROWS], F32, name="w_flipped")
+        nc.tensor.transpose(w_flipped[:], w_rows[:], identity[0:W_ROWS, 0:W_ROWS])
+        w_columns = held.tile([P, W_ROWS], F32, name="w_columns")
+        nc.scalar.copy(w_columns[:], w_flipped[:])
+
+        weights = held.tile([P, LIST], F32, name="weights")
+
+        def spread_w(piece):
+            for bank in range(piece * PIECE // BANK, (piece + 1) * PIECE // BANK):
+                spread = psum.tile([P, BANK], F32, name="spread")
+                for i in range(BANK // P):
+                    j = bank * (BANK // P) + i
+                    same_columns = w_columns[:, j : j + 1].to_broadcast([P, P])
+                    nc.tensor.transpose(spread[:, i * P : (i + 1) * P], same_columns, identity[:])
+                nc.scalar.copy(weights[:, bank * BANK : (bank + 1) * BANK], spread[:])
+
+        spread_w(0)
         for piece in range(PIECES):
             for block in range(BLOCKS):
                 product = work.tile([P, PIECE], F32, name="product")
@@ -57,6 +70,9 @@ def tile_lcn_kernel(tc, x, w, b, offs, out):
                         weights[:, node * FAN_IN : (node + nodes) * FAN_IN],
                         mybir.AluOpType.mult,
                     )
+
+                if block == 0 and piece + 1 < PIECES:
+                    spread_w(piece + 1)
 
                 by_neighbour = product[:].rearrange("p (q k) -> p q k", k=FAN_IN)
                 sums = psum.tile([P, P], F32, name="sums")

@@ -39,6 +39,9 @@ def tile_lcn_kernel(tc, x, w, b, offs, out):
         for block in range(BLOCKS):
             nc.sync.dma_start(tables[block][:], x[block * P : (block + 1) * P, :])
 
+        bias_rows = held.tile([P, PIECE_NODES], F32, name="bias_rows")
+        nc.sync.dma_start(bias_rows[:], b[0, OUT_NODES - PIECE_NODES : OUT_NODES].partition_broadcast(P))
+
         identity = held.tile([P, P], F32, name="identity")
         make_identity(nc, identity[:])
 
@@ -75,6 +78,18 @@ def tile_lcn_kernel(tc, x, w, b, offs, out):
                     spread_w(piece + 1)
 
                 by_neighbour = product[:].rearrange("p (q k) -> p q k", k=FAN_IN)
+                result = work.tile([P, P], F32, name="result")
+                to_out = out[block * P : (block + 1) * P, piece * PIECE_NODES : (piece + 1) * PIECE_NODES]
+
+                if (piece, block) == (PIECES - 1, BLOCKS - 1):
+                    own_sums = work.tile([P, P], F32, name="own_sums")
+                    nc.vector.reduce_sum(own_sums[:], by_neighbour, axis=mybir.AxisListType.X)
+                    with_bias = work.tile([P, P], F32, name="with_bias")
+                    nc.vector.tensor_add(with_bias[:], own_sums[:], bias_rows[:])
+                    nc.vector.tensor_scalar_max(result[:], with_bias[:], 0.0)
+                    nc.sync.dma_start(to_out, result[:])
+                    continue
+
                 sums = psum.tile([P, P], F32, name="sums")
                 for k in range(FAN_IN):
                     nc.tensor.matmul(
@@ -88,6 +103,5 @@ def tile_lcn_kernel(tc, x, w, b, offs, out):
 
                 turned = psum.tile([P, P], F32, name="turned")
                 nc.tensor.transpose(turned[:], active[:], identity[:])
-                result = work.tile([P, P], F32, name="result")
                 nc.scalar.copy(result[:], turned[:])
-                nc.sync.dma_start(out[block * P : (block + 1) * P, piece * PIECE_NODES : (piece + 1) * PIECE_NODES], result[:])
+                nc.sync.dma_start(to_out, result[:])

@@ -16,6 +16,8 @@ W_ROWS = LIST // P
 BANK = 512
 FIRST_CUT = ((0, PIECE_NODES // 4), (PIECE_NODES // 4, PIECE_NODES // 4), (PIECE_NODES // 2, PIECE_NODES // 2))
 WHOLE = ((0, PIECE_NODES),)
+HALF_NODES = PIECE_NODES // 2
+HALVES = ((0, HALF_NODES), (HALF_NODES, HALF_NODES))
 
 FLOPS = 2 * SAMPLES * LIST
 
@@ -65,7 +67,8 @@ def tile_lcn_kernel(tc, x, w, b, offs, out):
         for piece in range(PIECES):
             for block in range(BLOCKS):
                 product = work.tile([P, PIECE], F32, name="product")
-                for first_node, nodes in FIRST_CUT if (piece, block) == (0, 0) else WHOLE:
+                is_last = (piece, block) == (PIECES - 1, BLOCKS - 1)
+                for first_node, nodes in FIRST_CUT if (piece, block) == (0, 0) else HALVES if is_last else WHOLE:
                     node = piece * PIECE_NODES + first_node
                     nc.vector.tensor_tensor(
                         product[:, first_node * FAN_IN : (first_node + nodes) * FAN_IN],
@@ -81,9 +84,23 @@ def tile_lcn_kernel(tc, x, w, b, offs, out):
                 result = work.tile([P, P], F32, name="result")
                 to_out = out[block * P : (block + 1) * P, piece * PIECE_NODES : (piece + 1) * PIECE_NODES]
 
-                if (piece, block) == (PIECES - 1, BLOCKS - 1):
+                if is_last:
+                    every_eighth = product[:, 0 : HALF_NODES * FAN_IN].rearrange("p (q k) -> p q k", k=FAN_IN // 2)
+                    pair_sums = psum.tile([P, P], F32, name="sums")
+                    for k in range(FAN_IN // 2):
+                        nc.tensor.matmul(
+                            pair_sums[:], every_eighth[:, :, k], identity[:], start=(k == 0), stop=(k == FAN_IN // 2 - 1), is_transpose=True
+                        )
+                    pair_sums_sbuf = work.tile([P, P], F32, name="active")
+                    nc.scalar.copy(pair_sums_sbuf[:], pair_sums[:])
+                    pairs_back = psum.tile([P, P], F32, name="turned")
+                    nc.tensor.transpose(pairs_back[:], pair_sums_sbuf[:], identity[:])
+
                     own_sums = work.tile([P, P], F32, name="own_sums")
-                    nc.vector.reduce_sum(own_sums[:], by_neighbour, axis=mybir.AxisListType.X)
+                    nc.vector.reduce_sum(own_sums[:, HALF_NODES:], by_neighbour[:, HALF_NODES:, :], axis=mybir.AxisListType.X)
+                    nc.vector.reduce_sum(
+                        own_sums[:, 0:HALF_NODES], pairs_back[:].rearrange("p (d h) -> p d h", h=2), axis=mybir.AxisListType.X
+                    )
                     with_bias = work.tile([P, P], F32, name="with_bias")
                     nc.vector.tensor_add(with_bias[:], own_sums[:], bias_rows[:])
                     nc.vector.tensor_scalar_max(result[:], with_bias[:], 0.0)

@@ -14,6 +14,9 @@ PIECE = PIECE_NODES * FAN_IN
 PIECES = LIST // PIECE
 W_ROWS = LIST // P
 BANK = 512
+HALF_PIECE = PIECE // 2
+HALF_PIECES = LIST // HALF_PIECE
+AHEAD = 2 * BLOCKS
 FIRST_CUT = ((0, PIECE_NODES // 4), (PIECE_NODES // 4, PIECE_NODES // 4), (PIECE_NODES // 2, PIECE_NODES // 2))
 WHOLE = ((0, PIECE_NODES),)
 HALF_NODES = PIECE_NODES // 2
@@ -54,8 +57,8 @@ def tile_lcn_kernel(tc, x, w, b, offs, out):
 
         weights = held.tile([P, LIST], F32, name="weights")
 
-        def spread_w(piece):
-            for bank in range(piece * PIECE // BANK, (piece + 1) * PIECE // BANK):
+        def spread_w(half_piece):
+            for bank in range(half_piece * HALF_PIECE // BANK, (half_piece + 1) * HALF_PIECE // BANK):
                 spread = psum.tile([P, BANK], F32, name="spread")
                 for i in range(BANK // P):
                     j = bank * (BANK // P) + i
@@ -63,7 +66,8 @@ def tile_lcn_kernel(tc, x, w, b, offs, out):
                     nc.tensor.transpose(spread[:, i * P : (i + 1) * P], same_columns, identity[:])
                 nc.scalar.copy(weights[:, bank * BANK : (bank + 1) * BANK], spread[:])
 
-        spread_w(0)
+        for half_piece in range(AHEAD):
+            spread_w(half_piece)
         for piece in range(PIECES):
             for block in range(BLOCKS):
                 product = work.tile([P, PIECE], F32, name="product")
@@ -77,8 +81,9 @@ def tile_lcn_kernel(tc, x, w, b, offs, out):
                         mybir.AluOpType.mult,
                     )
 
-                if block == 0 and piece + 1 < PIECES:
-                    spread_w(piece + 1)
+                half_piece = piece * BLOCKS + block + AHEAD
+                if half_piece < HALF_PIECES:
+                    spread_w(half_piece)
 
                 by_neighbour = product[:].rearrange("p (q k) -> p q k", k=FAN_IN)
                 result = work.tile([P, P], F32, name="result")

@@ -35,14 +35,15 @@ def tile_lcn_kernel(tc, x, w, b, offs, out):
     ):
         w_rows = held.tile([W_ROWS, P], F32, name="w_rows")
         nc.scalar.dma_start(w_rows[:], w.rearrange("o (j p) -> (o j) p", p=P))
-        bias = held.tile([P, PIECES], F32, name="bias")
-        nc.scalar.dma_start(bias[:], b.rearrange("o (a p) -> p (a o)", p=P))
 
         offsets = held.tile([P, LIST // 16], U16, name="offsets")
         nc.sync.dma_start(offsets[:], offs)
         tables = [held.tile([P, IN_NODES], F32, name=f"table{block}") for block in range(BLOCKS)]
         for block in range(BLOCKS):
             nc.sync.dma_start(tables[block][:], x[block * P : (block + 1) * P, :])
+
+        bias = held.tile([P, PIECES], F32, name="bias")
+        nc.sync.dma_start(bias[:], b.rearrange("o (a p) -> p (a o)", p=P))
 
         bias_rows = held.tile([P, PIECE_NODES], F32, name="bias_rows")
         nc.sync.dma_start(bias_rows[:], b[0, OUT_NODES - PIECE_NODES : OUT_NODES].partition_broadcast(P))

@@ -34,13 +34,13 @@ def tile_lcn_kernel(tc, x, w, b, offs, out):
         tc.psum_pool(name="psum", bufs=2) as psum,
     ):
         w_rows = held.tile([W_ROWS, P], F32, name="w_rows")
-        nc.scalar.dma_start(w_rows[:], w.rearrange("o (j p) -> (o j) p", p=P))
+        nc.sync.dma_start(w_rows[:], w.rearrange("o (j p) -> (o j) p", p=P))
 
         offsets = held.tile([P, LIST // 16], U16, name="offsets")
         nc.sync.dma_start(offsets[:], offs)
         tables = [held.tile([P, IN_NODES], F32, name=f"table{block}") for block in range(BLOCKS)]
         for block in range(BLOCKS):
-            nc.sync.dma_start(tables[block][:], x[block * P : (block + 1) * P, :])
+            nc.scalar.dma_start(tables[block][:], x[block * P : (block + 1) * P, :])
 
         bias = held.tile([P, PIECES], F32, name="bias")
         nc.sync.dma_start(bias[:], b.rearrange("o (a p) -> p (a o)", p=P))

@@ -54,7 +54,7 @@ def tile_lcn_kernel(tc, x, w, b, offs, out):
         w_flipped = once.tile([P, W_ROWS], F32, name="w_flipped")
         nc.tensor.transpose(w_flipped[:], w_rows[:], identity[0:W_ROWS, 0:W_ROWS])
         w_columns = held.tile([P, W_ROWS], F32, name="w_columns")
-        nc.scalar.copy(w_columns[:], w_flipped[:])
+        nc.vector.tensor_copy(w_columns[:], w_flipped[:])
 
         weights = held.tile([P, LIST], F32, name="weights")
 
@@ -65,7 +65,10 @@ def tile_lcn_kernel(tc, x, w, b, offs, out):
                     j = bank * (BANK // P) + i
                     same_columns = w_columns[:, j : j + 1].to_broadcast([P, P])
                     nc.tensor.transpose(spread[:, i * P : (i + 1) * P], same_columns, identity[:])
-                nc.scalar.copy(weights[:, bank * BANK : (bank + 1) * BANK], spread[:])
+                if bank == 0:
+                    nc.vector.tensor_copy(weights[:, 0:BANK], spread[:])
+                else:
+                    nc.scalar.copy(weights[:, bank * BANK : (bank + 1) * BANK], spread[:])
 
         for half_piece in range(AHEAD):
             spread_w(half_piece)

@@ -43,10 +43,10 @@ def tile_lcn_kernel(tc, x, w, b, offs, out):
             nc.scalar.dma_start(tables[block][:], x[block * P : (block + 1) * P, :])
 
         bias = held.tile([P, PIECES], F32, name="bias")
-        nc.sync.dma_start(bias[:], b.rearrange("o (a p) -> p (a o)", p=P))
+        nc.scalar.dma_start(bias[:], b.rearrange("o (a p) -> p (a o)", p=P))
 
         bias_rows = held.tile([P, PIECE_NODES], F32, name="bias_rows")
-        nc.sync.dma_start(bias_rows[:], b[0, OUT_NODES - PIECE_NODES : OUT_NODES].partition_broadcast(P))
+        nc.scalar.dma_start(bias_rows[:], b[0, OUT_NODES - PIECE_NODES : OUT_NODES].partition_broadcast(P))
 
         identity = held.tile([P, P], F32, name="identity")
         make_identity(nc, identity[:])

import concourse.mybir as mybir
from concourse.masks import make_identity

F32 = mybir.dt.float32
U16 = mybir.dt.uint16

P = 128
SAMPLES, IN_NODES = 256, 2048
OUT_NODES, FAN_IN = 512, 16
BLOCKS = SAMPLES // P
LIST = OUT_NODES * FAN_IN
PIECE_NODES = P
PIECE = PIECE_NODES * FAN_IN
PIECES = LIST // PIECE
W_ROWS = LIST // P
BANK = 512
HALF_PIECE = PIECE // 2
HALF_PIECES = LIST // HALF_PIECE
AHEAD = 2 * BLOCKS
FIRST_CUT = ((0, PIECE_NODES // 4), (PIECE_NODES // 4, PIECE_NODES // 4), (PIECE_NODES // 2, PIECE_NODES // 2))
WHOLE = ((0, PIECE_NODES),)
HALF_NODES = PIECE_NODES // 2
HALVES = ((0, HALF_NODES), (HALF_NODES, HALF_NODES))

FLOPS = 2 * SAMPLES * LIST


def tile_lcn_kernel(tc, x, w, b, offs, out):
    nc = tc.nc
    with (
        tc.tile_pool(name="held", bufs=1) as held,
        tc.tile_pool(name="work", bufs=3) as work,
        tc.psum_pool(name="once", bufs=1) as once,
        tc.psum_pool(name="psum", bufs=2) as psum,
    ):
        w_rows = held.tile([W_ROWS, P], F32, name="w_rows")
        nc.sync.dma_start(w_rows[:], w.rearrange("o (j p) -> (o j) p", p=P))

        offsets = held.tile([P, LIST // 16], U16, name="offsets")
        nc.sync.dma_start(offsets[:], offs)
        tables = [held.tile([P, IN_NODES], F32, name=f"table{block}") for block in range(BLOCKS)]
        for block in range(BLOCKS):
            nc.scalar.dma_start(tables[block][:], x[block * P : (block + 1) * P, :])

        bias = held.tile([P, PIECES], F32, name="bias")
        nc.scalar.dma_start(bias[:], b.rearrange("o (a p) -> p (a o)", p=P))

        bias_rows = held.tile([P, PIECE_NODES], F32, name="bias_rows")
        nc.scalar.dma_start(bias_rows[:], b[0, OUT_NODES - PIECE_NODES : OUT_NODES].partition_broadcast(P))

        identity = held.tile([P, P], F32, name="identity")
        make_identity(nc, identity[:])

        w_flipped = once.tile([P, W_ROWS], F32, name="w_flipped")
        nc.tensor.transpose(w_flipped[:], w_rows[:], identity[0:W_ROWS, 0:W_ROWS])
        w_columns = held.tile([P, W_ROWS], F32, name="w_columns")
        nc.vector.tensor_copy(w_columns[:], w_flipped[:])

        weights = held.tile([P, LIST], F32, name="weights")

        def spread_w(half_piece):
            for bank in range(half_piece * HALF_PIECE // BANK, (half_piece + 1) * HALF_PIECE // BANK):
                spread = psum.tile([P, BANK], F32, name="spread")
                for i in range(BANK // P):
                    j = bank * (BANK // P) + i
                    same_columns = w_columns[:, j : j + 1].to_broadcast([P, P])
                    nc.tensor.transpose(spread[:, i * P : (i + 1) * P], same_columns, identity[:])
                if bank == 0:
                    nc.vector.tensor_copy(weights[:, 0:BANK], spread[:])
                else:
                    nc.scalar.copy(weights[:, bank * BANK : (bank + 1) * BANK], spread[:])

        for half_piece in range(AHEAD):
            spread_w(half_piece)
        for piece in range(PIECES):
            for block in range(BLOCKS):
                product = work.tile([P, PIECE], F32, name="product")
                is_last = (piece, block) == (PIECES - 1, BLOCKS - 1)
                for first_node, nodes in FIRST_CUT if (piece, block) == (0, 0) else HALVES if is_last else WHOLE:
                    node = piece * PIECE_NODES + first_node
                    nc.vector.tensor_tensor(
                        product[:, first_node * FAN_IN : (first_node + nodes) * FAN_IN],
                        tables[block][:].indirect(offsets[:, node : node + nodes]),
                        weights[:, node * FAN_IN : (node + nodes) * FAN_IN],
                        mybir.AluOpType.mult,
                    )

                half_piece = piece * BLOCKS + block + AHEAD
                if half_piece < HALF_PIECES:
                    spread_w(half_piece)

                by_neighbour = product[:].rearrange("p (q k) -> p q k", k=FAN_IN)
                result = work.tile([P, P], F32, name="result")
                to_out = out[block * P : (block + 1) * P, piece * PIECE_NODES : (piece + 1) * PIECE_NODES]

                if is_last:
                    every_eighth = product[:, 0 : HALF_NODES * FAN_IN].rearrange("p (q k) -> p q k", k=FAN_IN // 2)
                    pair_sums = psum.tile([P, P], F32, name="sums")
                    for k in range(FAN_IN // 2):
                        nc.tensor.matmul(
                            pair_sums[:], every_eighth[:, :, k], identity[:], start=(k == 0), stop=(k == FAN_IN // 2 - 1), is_transpose=True
                        )
                    pair_sums_sbuf = work.tile([P, P], F32, name="active")
                    nc.scalar.copy(pair_sums_sbuf[:], pair_sums[:])
                    pairs_back = psum.tile([P, P], F32, name="turned")
                    nc.tensor.transpose(pairs_back[:], pair_sums_sbuf[:], identity[:])

                    own_sums = work.tile([P, P], F32, name="own_sums")
                    nc.vector.reduce_sum(own_sums[:, HALF_NODES:], by_neighbour[:, HALF_NODES:, :], axis=mybir.AxisListType.X)
                    nc.vector.reduce_sum(
                        own_sums[:, 0:HALF_NODES], pairs_back[:].rearrange("p (d h) -> p d h", h=2), axis=mybir.AxisListType.X
                    )
                    with_bias = work.tile([P, P], F32, name="with_bias")
                    nc.vector.tensor_add(with_bias[:], own_sums[:], bias_rows[:])
                    nc.vector.tensor_scalar_max(result[:], with_bias[:], 0.0)
                    nc.sync.dma_start(to_out, result[:])
                    continue

                sums = psum.tile([P, P], F32, name="sums")
                for k in range(FAN_IN):
                    nc.tensor.matmul(
                        sums[:], by_neighbour[:, :, k], identity[:], start=(k == 0), stop=(k == FAN_IN - 1), is_transpose=True
                    )

                active = work.tile([P, P], F32, name="active")
                nc.scalar.activation(
                    active[:], sums[:], mybir.ActivationFunctionType.Relu, bias=bias[:, piece : piece + 1]
                )

                turned = psum.tile([P, P], F32, name="turned")
                nc.tensor.transpose(turned[:], active[:], identity[:])
                nc.scalar.copy(result[:], turned[:])
                nc.sync.dma_start(to_out, result[:])
